import numpy as np
import ml_dtypes


def mxq(x, axis, fmt="e4m3"):
    dtype, down = {"e4m3": (ml_dtypes.float8_e4m3fn, 7), "e5m2": (ml_dtypes.float8_e5m2, 14)}[fmt]
    v = np.moveaxis(np.asarray(x, np.float32).astype(ml_dtypes.bfloat16).astype(np.float64), axis, -1)
    blocks = v.reshape(v.shape[:-1] + (-1, 32))
    amax = np.abs(blocks).max(-1, keepdims=True)
    byte = np.maximum(np.where(amax > 0, np.frexp(amax)[1] - 1 + 127, 0) - down, 1)
    scale = np.exp2(byte - 127.0)
    codes = (blocks / scale).astype(np.float32).astype(dtype).astype(np.float64)
    return np.moveaxis((codes * scale).reshape(v.shape), -1, axis)


WIDE = False


def mx_kscale(k):
    if not WIDE:
        return np.ones(k)
    levels = np.array([10, -10, 5, -5, 0])
    if k % 512:
        return np.exp2(np.random.permutation(np.resize(levels, k // 32))).repeat(32)
    a = np.empty((k // 512, 16))
    for p in range(k // 512):
        a[p, :8] = np.random.permutation(np.resize(levels, 8))
        for g in range(8):
            far = levels[np.abs(levels - a[p, g]) >= 10]
            a[p, g + 8] = far[np.random.randint(len(far))]
    return np.exp2(a.ravel()).repeat(32)


BF16 = ml_dtypes.bfloat16


def bf(x):
    return np.asarray(x, np.float32).astype(BF16)


def f64(x):
    return np.asarray(x).astype(np.float64)


B, S, D, E = 1, 1024, 768, 2
K = E * D


def setup_inputs():
    s = mx_kscale(K)
    return {"att": bf(np.random.standard_normal((E, B, S, D)) * 0.3 * s.reshape(E, 1, 1, D)),
            "scene_reps": bf(np.random.standard_normal((B, S, D))),
            "Wo": bf(np.random.standard_normal((D, K)) * 2.0 / np.sqrt(K) / s[None, :]),
            "bo": bf(np.random.standard_normal(D) * 0.1),
            "gamma": bf(1.0 + np.random.standard_normal(D) * 0.1),
            "beta": bf(np.random.standard_normal(D) * 0.1)}


def core(att, scene_reps, Wo, bo, gamma, beta):
    cat = np.moveaxis(f64(att), 0, 2).reshape(B, S, K)
    fused = (mxq(cat, 2, "e4m3") @ mxq(f64(Wo), 1, "e4m3").T) + f64(bo)
    y = f64(scene_reps) + fused
    mu = y.mean(-1, keepdims=True)
    var = y.var(-1, keepdims=True)
    return (y - mu) / np.sqrt(var + 1e-5) * f64(gamma) + f64(beta)


def e4m3fn_bytes(y):
    return np.clip(np.asarray(y, np.float64), -448.0, 448.0).astype(np.float32).astype(ml_dtypes.float8_e4m3fn).view(np.uint8)


Y_SCALE = 220.0


def reference(att, scene_reps, Wo, bo, gamma, beta):
    out = core(att, scene_reps, Wo, bo, gamma, beta)
    return out, e4m3fn_bytes(out * Y_SCALE)

@@ -1,0 +1,287 @@
+from contextlib import ExitStack
+
+import concourse.mybir as mybir
+from concourse.masks import make_identity
+
+F32 = mybir.dt.float32
+BF16 = mybir.dt.bfloat16
+U32 = mybir.dt.uint32
+U8 = mybir.dt.uint8
+FP8X4 = mybir.dt.float8_e4m3fn_x4
+FP8 = mybir.dt.float8_e4m3fn
+ALU = mybir.AluOpType
+ACT = mybir.ActivationFunctionType
+
+P = 128
+TOKENS = 1024
+D = 768
+K = 1536
+PASSES = K // (4 * P)
+WORDS = 2 * P
+N_TILES = TOKENS // P
+W_PAIRS = D // (2 * P)
+MAIN = 512
+REST = D - MAIN
+Y_SCALE = 220.0
+EPS = 1e-5
+WARM_UPS = 3
+LAST_SPLIT = 448
+FLOPS = 2 * TOKENS * K * D
+
+
+def tile_heterogeneousgraphtransformer_pb_kernel(tc, att, scene_reps, Wo, bo, gamma, beta, out_0, out_1):
+    nc = tc.nc
+    cat_hbm = att.rearrange("e b s d -> (b s) e d")
+    res_hbm = scene_reps.flatten_outer_dims()
+    out0_hbm = out_0.flatten_outer_dims()
+    out1_hbm = out_1.flatten_outer_dims()
+
+    with ExitStack() as ctx:
+        const = ctx.enter_context(tc.tile_pool(name="const", bufs=1))
+        raw = ctx.enter_context(tc.tile_pool(name="raw", bufs=1))
+        grp = ctx.enter_context(tc.tile_pool(name="grp", bufs=3))
+        codes = ctx.enter_context(tc.tile_pool(name="codes", bufs=4))
+        wkeep = ctx.enter_context(tc.tile_pool(name="wkeep", bufs=1))
+        epi = ctx.enter_context(tc.tile_pool(name="epi", bufs=4))
+        small = ctx.enter_context(tc.tile_pool(name="small", bufs=6))
+        pconst = ctx.enter_context(tc.psum_pool(name="pconst", bufs=1))
+        work = ctx.enter_context(tc.psum_pool(name="work", bufs=6))
+        ctx.enter_context(tc.manual_schedule())
+
+        vec_rows = [const.tile([P, D], BF16, name="vec_row%d" % c) for c in range(3)]
+        nc.gpsimd.memset(vec_rows[2][:].bitcast(F32), 0.0)
+        ident = const.tile([P, P], F32, name="ident")
+        make_identity(nc, ident[:])
+        for c in range(2):
+            nc.vector.memset(vec_rows[c][:].bitcast(F32), 0.0)
+        one_col = const.tile([P, 1], F32, name="one_col")
+        nc.vector.memset(one_col[:], 1.0)
+        ones = const.tile([P, P], BF16, name="ones")
+        nc.vector.memset(ones[:], 1.0)
+        eps_col = const.tile([P, 1], F32, name="eps_col")
+        nc.vector.memset(eps_col[:], EPS)
+        table_warm = const.tile([P, 1], F32, name="table_warm")
+        nc.scalar.activation(out=table_warm[:], in_=one_col[:], func=ACT.Abs_reciprocal_sqrt)
+
+        cat_raw = [raw.tile([P, K], BF16, name="cat%d" % i) for i in range(N_TILES)]
+        wo_raw = [raw.tile([P, K], BF16, name="wo%d" % j) for j in range(2 * W_PAIRS)]
+        res_raw = [raw.tile([P, D], BF16, name="res%d" % i) for i in range(N_TILES)]
+
+        def load_cat(i):
+            nc.sync.dma_start(out=cat_raw[i][:].rearrange("p (e d) -> p e d", e=2), in_=cat_hbm[i * P:(i + 1) * P, :, :])
+
+        def load_res(i):
+            nc.sync.dma_start(out=res_raw[i][:], in_=res_hbm[i * P:(i + 1) * P, :])
+
+        load_cat(0)
+        load_res(0)
+        load_res(1)
+        for c, vec in enumerate((bo, gamma, beta)):
+            nc.sync.dma_start(out=vec_rows[c][0:1, :], in_=vec.rearrange("(o d) -> o d", o=1))
+        for j in range(2 * W_PAIRS):
+            nc.sync.dma_start(out=wo_raw[j][:], in_=Wo[j * P:(j + 1) * P, :])
+        load_cat(1)
+        for i in range(2, N_TILES):
+            load_cat(i)
+            load_res(i)
+
+        def turn(dst, words, g, u):
+            nc.tensor.transpose(dst, words[:, WORDS * g + u:WORDS * (g + 1):2], ident[:])
+
+        def interleaved(bank):
+            return bank.rearrange("p (a u) r -> p a r u", u=2)
+
+        def cat_transposes(i):
+            words = cat_raw[i][:].bitcast(F32)
+            bank_a = work.tile([P, 4, P], F32, name="bank_a", tag="bank")
+            for g in (0, 1):
+                for u in (0, 1):
+                    turn(bank_a[:, 2 * g + u, :], words, g, u)
+            bank_b = work.tile([P, 4, P], F32, name="bank_b", tag="bank")
+            for u in (0, 1):
+                turn(bank_b[:, u, :], words, 2, u)
+            return bank_a, bank_b
+
+        def cat_copies(banks):
+            bank_a, bank_b = banks
+            grouped_a = grp.tile([P, 2, P, 4], BF16, name="grouped_a", tag="grouped_a", align_bytes=64)
+            grouped_b = grp.tile([P, 1, P, 4], BF16, name="grouped_b", tag="grouped_b", align_bytes=64)
+            nc.scalar.copy(out=grouped_a[:].bitcast(F32), in_=interleaved(bank_a[:]))
+            nc.scalar.copy(out=grouped_b[:].bitcast(F32), in_=interleaved(bank_b[:, 0:2, :]))
+            return grouped_a, grouped_b
+
+        def cat_quantize(grouped):
+            grouped_a, grouped_b = grouped
+            codes_a = codes.tile([P, 2 * P], U32, name="codes_a", tag="codes_a", align_bytes=64)
+            scales_a = codes.tile([P, 2 * P], U8, name="scales_a", tag="scales_a", align_bytes=64)
+            codes_b = codes.tile([P, P], U32, name="codes_b", tag="codes_b", align_bytes=64)
+            scales_b = codes.tile([P, P], U8, name="scales_b", tag="scales_b", align_bytes=64)
+            nc.vector.quantize_mx(out=codes_a[:].bitcast(FP8X4), scales=scales_a[:], in_=grouped_a[:].rearrange("p g r t -> p (g r t)"))
+            nc.vector.quantize_mx(out=codes_b[:].bitcast(FP8X4), scales=scales_b[:], in_=grouped_b[:].rearrange("p g r t -> p (g r t)"))
+            return ((codes_a[:, 0:P], scales_a[:, 0:P]), (codes_a[:, P:2 * P], scales_a[:, P:2 * P]), (codes_b[:], scales_b[:]))
+
+        w_codes = [wkeep.tile([P, D], U32, name="w_codes%d" % g, align_bytes=64) for g in range(PASSES)]
+        w_scales = [wkeep.tile([P, D], U8, name="w_scales%d" % g, align_bytes=64) for g in range(PASSES)]
+
+        def w_pair(pair):
+            banks = [work.tile([P, 4, P], F32, name="bank_w%d" % g, tag="bank") for g in range(PASSES)]
+            for half in (0, 1):
+                words = wo_raw[2 * pair + half][:].bitcast(F32)
+                for g in range(PASSES):
+                    for u in (0, 1):
+                        turn(banks[g][:, 2 * half + u, :], words, g, u)
+            grouped = [grp.tile([P, 2, P, 4], BF16, name="grouped_w%d" % g, tag="grouped_w", bufs=4, align_bytes=64) for g in range(PASSES)]
+            for g in range(PASSES):
+                nc.scalar.copy(out=grouped[g][:].bitcast(F32), in_=interleaved(banks[g][:]))
+            cols = slice(pair * 2 * P, (pair + 1) * 2 * P)
+            for g in range(PASSES):
+                nc.vector.quantize_mx(out=w_codes[g][:, cols].bitcast(FP8X4), scales=w_scales[g][:, cols], in_=grouped[g][:].rearrange("p h r t -> p (h r t)"))
+
+        cat_mx = {}
+        sum_main = {}
+        sum_rest = {}
+
+        def mx_group(i, lo, hi, acc):
+            for g in range(PASSES):
+                nc.tensor.matmul_mx(
+                    out=acc,
+                    lhsT=cat_mx[i][g][0].bitcast(FP8X4),
+                    lhsT_scale=cat_mx[i][g][1],
+                    rhs=w_codes[g][:, lo:hi].bitcast(FP8X4),
+                    rhs_scale=w_scales[g][:, lo:hi],
+                    start=(g == 0),
+                    stop=(g == PASSES - 1),
+                )
+
+        def mx_main(i):
+            bank = work.tile([P, MAIN], F32, name="bank_main", tag="bank")
+            sum_main[i] = bank[:]
+            mx_group(i, 0, MAIN, sum_main[i])
+
+        def mx_rest(i):
+            if i % 2 == 0:
+                bank = work.tile([P, 2 * REST], F32, name="bank_rest", tag="bank")
+                sum_rest[i] = bank[:, 0:REST]
+                sum_rest[i + 1] = bank[:, REST:2 * REST]
+            mx_group(i, MAIN, D, sum_rest[i])
+
+        gamma_ps = pconst.tile([P, D], BF16, name="gamma_ps")
+        beta_ps = pconst.tile([P, D], BF16, name="beta_ps")
+        bias_sb = const.tile([P, D], BF16, name="bias_sb")
+        res_bias = [raw.tile([P, D], F32, name="res_bias%d" % i) for i in range(N_TILES)]
+
+        def spread(dst, c):
+            nc.tensor.matmul(out=dst[:, 0:MAIN], lhsT=ones[:], rhs=vec_rows[c][:, 0:MAIN], start=True, stop=True)
+            nc.tensor.matmul(out=dst[:, MAIN:D], lhsT=ones[:], rhs=vec_rows[c][:, MAIN:D], start=True, stop=True)
+
+        def warm_up():
+            scratch = work.tile([P, MAIN], F32, name="scratch", tag="bank")
+            for w in range(WARM_UPS):
+                nc.tensor.matmul(out=scratch[:, 0:P], lhsT=ident[:], rhs=ident[:], start=True, stop=True)
+
+        def bias_spread():
+            bias_ps = work.tile([P, D], BF16, name="bias_ps", tag="bank")
+            spread(bias_ps, 0)
+            nc.scalar.copy(out=bias_sb[:], in_=bias_ps[:])
+            for i in (0, 1):
+                nc.vector.tensor_tensor(out=res_bias[i][:], in0=bias_ps[:], in1=res_raw[i][:], op=ALU.add)
+
+        def pool_res_bias(i):
+            token = small.tile([P, 1], U32, name="token", tag="token")
+            nc.gpsimd.tensor_copy(out=token[:], in_=cat_mx[i][PASSES - 1][0][:, 0:1])
+            nc.gpsimd.tensor_tensor(out=res_bias[i][:], in0=res_raw[i][:], in1=bias_sb[:], op=ALU.add)
+
+        y = {}
+        row_sums = {}
+        neg_mean = {}
+        rstd = {}
+        scaled = {}
+        result = {}
+
+        def add_residual(i):
+            y[i] = epi.tile([P, D], F32, name="y", tag="y")
+            row_sums[i] = small.tile([P, 2], F32, name="row_sums", tag="row_sums")
+            nc.vector.scalar_tensor_tensor(out=y[i][:, 0:MAIN], in0=sum_main[i], scalar=1.0, in1=res_bias[i][:, 0:MAIN], op0=ALU.mult, op1=ALU.add, accum_out=row_sums[i][:, 0:1])
+            nc.vector.scalar_tensor_tensor(out=y[i][:, MAIN:D], in0=sum_rest[i], scalar=1.0, in1=res_bias[i][:, MAIN:D], op0=ALU.mult, op1=ALU.add, accum_out=row_sums[i][:, 1:2])
+
+        def mean(i):
+            neg_mean[i] = small.tile([P, 1], F32, name="neg_mean", tag="neg_mean")
+            unused = small.tile([P, 2], F32, name="unused2", tag="unused2")
+            nc.scalar.activation(out=unused[:], in_=row_sums[i][:], func=ACT.Copy, scale=-1.0 / D, accum_out=neg_mean[i][:, 0:1])
+
+        def variance(i):
+            unused = epi.tile([P, D], BF16, name="unused", tag="unused")
+            squares = small.tile([P, 1], F32, name="squares", tag="squares")
+            nc.scalar.activation(out=unused[:], in_=y[i][:], func=ACT.Square, bias=neg_mean[i][:, 0:1], scale=1.0, accum_out=squares[:, 0:1])
+            rstd[i] = small.tile([P, 1], F32, name="rstd", tag="rstd")
+            nc.scalar.activation(out=rstd[i][:], in_=squares[:], func=ACT.Abs_reciprocal_sqrt, bias=eps_col[:, 0:1], scale=1.0 / D)
+
+        def times_gamma(i):
+            scaled[i] = epi.tile([P, D], F32, name="scaled", tag="scaled")
+            nc.vector.scalar_tensor_tensor(out=scaled[i][:], in0=y[i][:], scalar=neg_mean[i][:, 0:1], in1=gamma_ps[:], op0=ALU.add, op1=ALU.mult)
+
+        def plus_beta(i, lo, hi):
+            if lo == 0:
+                result[i] = epi.tile([P, D], F32, name="result", tag="result")
+            nc.vector.scalar_tensor_tensor(out=result[i][:, lo:hi], in0=scaled[i][:, lo:hi], scalar=rstd[i][:, 0:1], in1=beta_ps[:, lo:hi], op0=ALU.mult, op1=ALU.add)
+            nc.sync.dma_start(out=out0_hbm[i * P:(i + 1) * P, lo:hi], in_=result[i][:, lo:hi])
+
+        def cast(i, lo, hi, on_vector):
+            fp8 = epi.tile([P, hi - lo], FP8, name="fp8", tag="fp8")
+            if on_vector:
+                nc.vector.tensor_scalar(out=fp8[:], in0=result[i][:, lo:hi], scalar1=Y_SCALE, scalar2=None, op0=ALU.mult, saturate=False)
+            else:
+                nc.scalar.activation(out=fp8[:], in_=result[i][:, lo:hi], func=ACT.Copy, scale=Y_SCALE, saturate=False)
+            return fp8
+
+        def store_bytes(i, lo, hi, fp8):
+            nc.sync.dma_start(out=out1_hbm[i * P:(i + 1) * P, lo:hi], in_=fp8[:].bitcast(U8))
+
+        warm_up()
+        grouped_0 = cat_copies(cat_transposes(0))
+        bias_spread()
+        cat_mx[0] = cat_quantize(grouped_0)
+        w_pair(0)
+        spread(gamma_ps, 1)
+        w_pair(1)
+        spread(beta_ps, 2)
+        w_pair(2)
+        banks_1 = cat_transposes(1)
+        mx_main(0)
+        mx_rest(0)
+        banks_2 = cat_transposes(2)
+        grouped = {1: cat_copies(banks_1)}
+
+        for i in range(N_TILES + 1):
+            if i < N_TILES:
+                add_residual(i)
+            if i == 0:
+                cat_mx[1] = cat_quantize(grouped[1])
+            if i + 1 < N_TILES:
+                mx_main(i + 1)
+                mx_rest(i + 1)
+            if i + 3 < N_TILES:
+                banks_ahead = cat_transposes(i + 3)
+            if i < N_TILES:
+                mean(i)
+            if i == 0:
+                grouped[2] = cat_copies(banks_2)
+            if 1 <= i < N_TILES:
+                plus_beta(i - 1, 0, D)
+            if i < N_TILES:
+                variance(i)
+            if 1 <= i < N_TILES:
+                store_bytes(i - 1, 0, D, cast(i - 1, 0, D, False))
+            if i == N_TILES:
+                plus_beta(i - 1, 0, LAST_SPLIT)
+                fp8_first = cast(i - 1, 0, LAST_SPLIT, False)
+                plus_beta(i - 1, LAST_SPLIT, D)
+                store_bytes(i - 1, LAST_SPLIT, D, cast(i - 1, LAST_SPLIT, D, True))
+                store_bytes(i - 1, 0, LAST_SPLIT, fp8_first)
+            if i < N_TILES:
+                times_gamma(i)
+            if i + 2 < N_TILES:
+                cat_mx[i + 2] = cat_quantize(grouped[i + 2])
+                pool_res_bias(i + 2)
+            if i + 3 < N_TILES:
+                grouped[i + 3] = cat_copies(banks_ahead)

@@ -159,10 +159,8 @@ def tile_heterogeneousgraphtransformer_pb_kernel(tc, att, scene_reps, Wo, bo, ga
             mx_group(i, 0, MAIN, sum_main[i])
 
         def mx_rest(i):
-            if i % 2 == 0:
-                bank = work.tile([P, 2 * REST], F32, name="bank_rest", tag="bank")
-                sum_rest[i] = bank[:, 0:REST]
-                sum_rest[i + 1] = bank[:, REST:2 * REST]
+            bank = work.tile([P, REST], F32, name="bank_rest", tag="bank")
+            sum_rest[i] = bank[:]
             mx_group(i, MAIN, D, sum_rest[i])
 
         gamma_ps = pconst.tile([P, D], BF16, name="gamma_ps")
@@ -278,10 +276,12 @@ def tile_heterogeneousgraphtransformer_pb_kernel(tc, att, scene_reps, Wo, bo, ga
                 plus_beta(i - 1, LAST_SPLIT, D)
                 store_bytes(i - 1, LAST_SPLIT, D, cast(i - 1, LAST_SPLIT, D, True))
                 store_bytes(i - 1, 0, LAST_SPLIT, fp8_first)
-            if i < N_TILES:
+            if i == 0:
                 times_gamma(i)
             if i + 2 < N_TILES:
                 cat_mx[i + 2] = cat_quantize(grouped[i + 2])
                 pool_res_bias(i + 2)
+            if 1 <= i < N_TILES:
+                times_gamma(i)
             if i + 3 < N_TILES:
                 grouped[i + 3] = cat_copies(banks_ahead)

@@ -123,13 +123,15 @@ def tile_heterogeneousgraphtransformer_pb_kernel(tc, att, scene_reps, Wo, bo, ga
         w_codes = [wkeep.tile([P, D], U32, name="w_codes%d" % g, align_bytes=64) for g in range(PASSES)]
         w_scales = [wkeep.tile([P, D], U8, name="w_scales%d" % g, align_bytes=64) for g in range(PASSES)]
 
-        def w_pair(pair):
+        def w_pair(pair, between=None):
             banks = [work.tile([P, 4, P], F32, name="bank_w%d" % g, tag="bank") for g in range(PASSES)]
             for half in (0, 1):
                 words = wo_raw[2 * pair + half][:].bitcast(F32)
                 for g in range(PASSES):
                     for u in (0, 1):
                         turn(banks[g][:, 2 * half + u, :], words, g, u)
+                if half == 0 and between is not None:
+                    between()
             grouped = [grp.tile([P, 2, P, 4], BF16, name="grouped_w%d" % g, tag="grouped_w", bufs=4, align_bytes=64) for g in range(PASSES)]
             for g in range(PASSES):
                 nc.scalar.copy(out=grouped[g][:].bitcast(F32), in_=interleaved(banks[g][:]))
@@ -242,8 +244,7 @@ def tile_heterogeneousgraphtransformer_pb_kernel(tc, att, scene_reps, Wo, bo, ga
         w_pair(0)
         spread(gamma_ps, 1)
         w_pair(1)
-        spread(beta_ps, 2)
-        w_pair(2)
+        w_pair(2, lambda: spread(beta_ps, 2))
         banks_1 = cat_transposes(1)
         mx_main(0)
         mx_rest(0)

@@ -26,6 +26,8 @@ Y_SCALE = 220.0
 EPS = 1e-5
 WARM_UPS = 3
 LAST_SPLIT = 448
+HELPED = (5, 6)
+HELP_LO = 512
 FLOPS = 2 * TOKENS * K * D
 
 
@@ -84,6 +86,10 @@ def tile_heterogeneousgraphtransformer_pb_kernel(tc, att, scene_reps, Wo, bo, ga
         for i in range(2, N_TILES):
             load_cat(i)
             load_res(i)
+        gamma_sb = const.tile([P, D - HELP_LO], BF16, name="gamma_sb")
+        beta_sb = const.tile([P, D - HELP_LO], BF16, name="beta_sb")
+        nc.sync.dma_start(out=gamma_sb[:], in_=gamma[HELP_LO:D].partition_broadcast(P))
+        nc.sync.dma_start(out=beta_sb[:], in_=beta[HELP_LO:D].partition_broadcast(P))
 
         def turn(dst, words, g, u):
             nc.tensor.transpose(dst, words[:, WORDS * g + u:WORDS * (g + 1):2], ident[:])
@@ -218,13 +224,22 @@ def tile_heterogeneousgraphtransformer_pb_kernel(tc, att, scene_reps, Wo, bo, ga
 
         def times_gamma(i):
             scaled[i] = epi.tile([P, D], F32, name="scaled", tag="scaled")
-            nc.vector.scalar_tensor_tensor(out=scaled[i][:], in0=y[i][:], scalar=neg_mean[i][:, 0:1], in1=gamma_ps[:], op0=ALU.add, op1=ALU.mult)
+            hi = HELP_LO if i in HELPED else D
+            nc.vector.scalar_tensor_tensor(out=scaled[i][:, 0:hi], in0=y[i][:, 0:hi], scalar=neg_mean[i][:, 0:1], in1=gamma_ps[:, 0:hi], op0=ALU.add, op1=ALU.mult)
 
         def plus_beta(i, lo, hi):
             if lo == 0:
                 result[i] = epi.tile([P, D], F32, name="result", tag="result")
             nc.vector.scalar_tensor_tensor(out=result[i][:, lo:hi], in0=scaled[i][:, lo:hi], scalar=rstd[i][:, 0:1], in1=beta_ps[:, lo:hi], op0=ALU.mult, op1=ALU.add)
             nc.sync.dma_start(out=out0_hbm[i * P:(i + 1) * P, lo:hi], in_=result[i][:, lo:hi])
+
+        def pool_help(i):
+            normed = epi.tile([P, D - HELP_LO], F32, name="normed", tag="normed", bufs=2)
+            gained = epi.tile([P, D - HELP_LO], F32, name="gained", tag="gained", bufs=2)
+            nc.gpsimd.tensor_scalar(out=normed[:], in0=y[i][:, HELP_LO:D], scalar1=neg_mean[i][:, 0:1], scalar2=rstd[i][:, 0:1], op0=ALU.add, op1=ALU.mult)
+            nc.gpsimd.tensor_tensor(out=gained[:], in0=normed[:], in1=gamma_sb[:], op=ALU.mult)
+            nc.gpsimd.tensor_tensor(out=result[i][:, HELP_LO:D], in0=gained[:], in1=beta_sb[:], op=ALU.add)
+            nc.sync.dma_start(out=out0_hbm[i * P:(i + 1) * P, HELP_LO:D], in_=result[i][:, HELP_LO:D])
 
         def cast(i, lo, hi, on_vector):
             fp8 = epi.tile([P, hi - lo], FP8, name="fp8", tag="fp8")
@@ -266,11 +281,16 @@ def tile_heterogeneousgraphtransformer_pb_kernel(tc, att, scene_reps, Wo, bo, ga
             if i == 0:
                 grouped[2] = cat_copies(banks_2)
             if 1 <= i < N_TILES:
-                plus_beta(i - 1, 0, D)
+                plus_beta(i - 1, 0, HELP_LO if i - 1 in HELPED else D)
             if i < N_TILES:
                 variance(i)
             if 1 <= i < N_TILES:
-                store_bytes(i - 1, 0, D, cast(i - 1, 0, D, False))
+                hi = HELP_LO if i - 1 in HELPED else D
+                store_bytes(i - 1, 0, hi, cast(i - 1, 0, hi, False))
+            if i - 1 in HELPED:
+                pool_help(i - 1)
+            if i - 2 in HELPED:
+                store_bytes(i - 2, HELP_LO, D, cast(i - 2, HELP_LO, D, False))
             if i == N_TILES:
                 plus_beta(i - 1, 0, LAST_SPLIT)
                 fp8_first = cast(i - 1, 0, LAST_SPLIT, False)

@@ -26,7 +26,7 @@ Y_SCALE = 220.0
 EPS = 1e-5
 WARM_UPS = 3
 LAST_SPLIT = 448
-HELPED = (5, 6)
+HELPED = (5,)
 HELP_LO = 512
 FLOPS = 2 * TOKENS * K * D
 

@@ -77,11 +77,11 @@ def tile_heterogeneousgraphtransformer_pb_kernel(tc, att, scene_reps, Wo, bo, ga
 
         load_cat(0)
         load_res(0)
-        load_res(1)
         for c, vec in enumerate((bo, gamma, beta)):
             nc.sync.dma_start(out=vec_rows[c][0:1, :], in_=vec.rearrange("(o d) -> o d", o=1))
         for j in range(2 * W_PAIRS):
             nc.sync.dma_start(out=wo_raw[j][:], in_=Wo[j * P:(j + 1) * P, :])
+        load_res(1)
         load_cat(1)
         for i in range(2, N_TILES):
             load_cat(i)
@@ -129,7 +129,7 @@ def tile_heterogeneousgraphtransformer_pb_kernel(tc, att, scene_reps, Wo, bo, ga
         w_codes = [wkeep.tile([P, D], U32, name="w_codes%d" % g, align_bytes=64) for g in range(PASSES)]
         w_scales = [wkeep.tile([P, D], U8, name="w_scales%d" % g, align_bytes=64) for g in range(PASSES)]
 
-        def w_pair(pair, between=None):
+        def w_pair(pair, between=None, before_quantize=None):
             banks = [work.tile([P, 4, P], F32, name="bank_w%d" % g, tag="bank") for g in range(PASSES)]
             for half in (0, 1):
                 words = wo_raw[2 * pair + half][:].bitcast(F32)
@@ -142,6 +142,8 @@ def tile_heterogeneousgraphtransformer_pb_kernel(tc, att, scene_reps, Wo, bo, ga
             for g in range(PASSES):
                 nc.scalar.copy(out=grouped[g][:].bitcast(F32), in_=interleaved(banks[g][:]))
             cols = slice(pair * 2 * P, (pair + 1) * 2 * P)
+            if before_quantize is not None:
+                before_quantize()
             for g in range(PASSES):
                 nc.vector.quantize_mx(out=w_codes[g][:, cols].bitcast(FP8X4), scales=w_scales[g][:, cols], in_=grouped[g][:].rearrange("p h r t -> p (h r t)"))
 
@@ -189,8 +191,7 @@ def tile_heterogeneousgraphtransformer_pb_kernel(tc, att, scene_reps, Wo, bo, ga
             bias_ps = work.tile([P, D], BF16, name="bias_ps", tag="bank")
             spread(bias_ps, 0)
             nc.scalar.copy(out=bias_sb[:], in_=bias_ps[:])
-            for i in (0, 1):
-                nc.vector.tensor_tensor(out=res_bias[i][:], in0=bias_ps[:], in1=res_raw[i][:], op=ALU.add)
+            nc.vector.tensor_tensor(out=res_bias[0][:], in0=bias_ps[:], in1=res_raw[0][:], op=ALU.add)
 
         def pool_res_bias(i):
             token = small.tile([P, 1], U32, name="token", tag="token")
@@ -259,7 +260,7 @@ def tile_heterogeneousgraphtransformer_pb_kernel(tc, att, scene_reps, Wo, bo, ga
         w_pair(0)
         spread(gamma_ps, 1)
         w_pair(1)
-        w_pair(2, lambda: spread(beta_ps, 2))
+        w_pair(2, lambda: spread(beta_ps, 2), lambda: nc.vector.tensor_tensor(out=res_bias[1][:], in0=res_raw[1][:], in1=bias_sb[:], op=ALU.add))
         banks_1 = cat_transposes(1)
         mx_main(0)
         mx_rest(0)

@@ -51,9 +51,9 @@ def tile_heterogeneousgraphtransformer_pb_kernel(tc, att, scene_reps, Wo, bo, ga
         ctx.enter_context(tc.manual_schedule())
 
         vec_rows = [const.tile([P, D], BF16, name="vec_row%d" % c) for c in range(3)]
-        nc.gpsimd.memset(vec_rows[2][:].bitcast(F32), 0.0)
         ident = const.tile([P, P], F32, name="ident")
         make_identity(nc, ident[:])
+        nc.gpsimd.memset(vec_rows[2][:].bitcast(F32), 0.0)
         for c in range(2):
             nc.vector.memset(vec_rows[c][:].bitcast(F32), 0.0)
         one_col = const.tile([P, 1], F32, name="one_col")
@@ -75,12 +75,15 @@ def tile_heterogeneousgraphtransformer_pb_kernel(tc, att, scene_reps, Wo, bo, ga
         def load_res(i):
             nc.sync.dma_start(out=res_raw[i][:], in_=res_hbm[i * P:(i + 1) * P, :])
 
-        load_cat(0)
-        load_res(0)
-        for c, vec in enumerate((bo, gamma, beta)):
-            nc.sync.dma_start(out=vec_rows[c][0:1, :], in_=vec.rearrange("(o d) -> o d", o=1))
+        for e in (0, 1):
+            nc.sync.dma_start(out=cat_raw[0][:, e * D:(e + 1) * D], in_=cat_hbm[0:P, e, :])
         for j in range(2 * W_PAIRS):
             nc.sync.dma_start(out=wo_raw[j][:], in_=Wo[j * P:(j + 1) * P, :])
+            if j == 0:
+                for c, vec in enumerate((bo, gamma, beta)):
+                    nc.sync.dma_start(out=vec_rows[c][0:1, :], in_=vec.rearrange("(o d) -> o d", o=1))
+            if j == 1:
+                load_res(0)
         load_res(1)
         load_cat(1)
         for i in range(2, N_TILES):
@@ -255,9 +258,8 @@ def tile_heterogeneousgraphtransformer_pb_kernel(tc, att, scene_reps, Wo, bo, ga
 
         warm_up()
         grouped_0 = cat_copies(cat_transposes(0))
-        bias_spread()
         cat_mx[0] = cat_quantize(grouped_0)
-        w_pair(0)
+        w_pair(0, bias_spread)
         spread(gamma_ps, 1)
         w_pair(1)
         w_pair(2, lambda: spread(beta_ps, 2), lambda: nc.vector.tensor_tensor(out=res_bias[1][:], in0=res_raw[1][:], in1=bias_sb[:], op=ALU.add))

@@ -246,7 +246,7 @@ def tile_heterogeneousgraphtransformer_pb_kernel(tc, att, scene_reps, Wo, bo, ga
             nc.sync.dma_start(out=out0_hbm[i * P:(i + 1) * P, HELP_LO:D], in_=result[i][:, HELP_LO:D])
 
         def cast(i, lo, hi, on_vector):
-            fp8 = epi.tile([P, hi - lo], FP8, name="fp8", tag="fp8")
+            fp8 = epi.tile([P, hi - lo], FP8, name="fp8", tag="fp8", bufs=8)
             if on_vector:
                 nc.vector.tensor_scalar(out=fp8[:], in0=result[i][:, lo:hi], scalar1=Y_SCALE, scalar2=None, op0=ALU.mult, saturate=False)
             else:

from contextlib import ExitStack

import concourse.mybir as mybir
from concourse.masks import make_identity

F32 = mybir.dt.float32
BF16 = mybir.dt.bfloat16
U32 = mybir.dt.uint32
U8 = mybir.dt.uint8
FP8X4 = mybir.dt.float8_e4m3fn_x4
FP8 = mybir.dt.float8_e4m3fn
ALU = mybir.AluOpType
ACT = mybir.ActivationFunctionType

P = 128
TOKENS = 1024
D = 768
K = 1536
PASSES = K // (4 * P)
WORDS = 2 * P
N_TILES = TOKENS // P
W_PAIRS = D // (2 * P)
MAIN = 512
REST = D - MAIN
Y_SCALE = 220.0
EPS = 1e-5
WARM_UPS = 3
LAST_SPLIT = 448
HELPED = (5,)
HELP_LO = 512
FLOPS = 2 * TOKENS * K * D


def tile_heterogeneousgraphtransformer_pb_kernel(tc, att, scene_reps, Wo, bo, gamma, beta, out_0, out_1):
    nc = tc.nc
    cat_hbm = att.rearrange("e b s d -> (b s) e d")
    res_hbm = scene_reps.flatten_outer_dims()
    out0_hbm = out_0.flatten_outer_dims()
    out1_hbm = out_1.flatten_outer_dims()

    with ExitStack() as ctx:
        const = ctx.enter_context(tc.tile_pool(name="const", bufs=1))
        raw = ctx.enter_context(tc.tile_pool(name="raw", bufs=1))
        grp = ctx.enter_context(tc.tile_pool(name="grp", bufs=3))
        codes = ctx.enter_context(tc.tile_pool(name="codes", bufs=4))
        wkeep = ctx.enter_context(tc.tile_pool(name="wkeep", bufs=1))
        epi = ctx.enter_context(tc.tile_pool(name="epi", bufs=4))
        small = ctx.enter_context(tc.tile_pool(name="small", bufs=6))
        pconst = ctx.enter_context(tc.psum_pool(name="pconst", bufs=1))
        work = ctx.enter_context(tc.psum_pool(name="work", bufs=6))
        ctx.enter_context(tc.manual_schedule())

        vec_rows = [const.tile([P, D], BF16, name="vec_row%d" % c) for c in range(3)]
        ident = const.tile([P, P], F32, name="ident")
        make_identity(nc, ident[:])
        nc.gpsimd.memset(vec_rows[2][:].bitcast(F32), 0.0)
        for c in range(2):
            nc.vector.memset(vec_rows[c][:].bitcast(F32), 0.0)
        one_col = const.tile([P, 1], F32, name="one_col")
        nc.vector.memset(one_col[:], 1.0)
        ones = const.tile([P, P], BF16, name="ones")
        nc.vector.memset(ones[:], 1.0)
        eps_col = const.tile([P, 1], F32, name="eps_col")
        nc.vector.memset(eps_col[:], EPS)
        table_warm = const.tile([P, 1], F32, name="table_warm")
        nc.scalar.activation(out=table_warm[:], in_=one_col[:], func=ACT.Abs_reciprocal_sqrt)

        cat_raw = [raw.tile([P, K], BF16, name="cat%d" % i) for i in range(N_TILES)]
        wo_raw = [raw.tile([P, K], BF16, name="wo%d" % j) for j in range(2 * W_PAIRS)]
        res_raw = [raw.tile([P, D], BF16, name="res%d" % i) for i in range(N_TILES)]

        def load_cat(i):
            nc.sync.dma_start(out=cat_raw[i][:].rearrange("p (e d) -> p e d", e=2), in_=cat_hbm[i * P:(i + 1) * P, :, :])

        def load_res(i):
            nc.sync.dma_start(out=res_raw[i][:], in_=res_hbm[i * P:(i + 1) * P, :])

        for e in (0, 1):
            nc.sync.dma_start(out=cat_raw[0][:, e * D:(e + 1) * D], in_=cat_hbm[0:P, e, :])
        for j in range(2 * W_PAIRS):
            nc.sync.dma_start(out=wo_raw[j][:], in_=Wo[j * P:(j + 1) * P, :])
            if j == 0:
                for c, vec in enumerate((bo, gamma, beta)):
                    nc.sync.dma_start(out=vec_rows[c][0:1, :], in_=vec.rearrange("(o d) -> o d", o=1))
            if j == 1:
                load_res(0)
        load_res(1)
        load_cat(1)
        for i in range(2, N_TILES):
            load_cat(i)
            load_res(i)
        gamma_sb = const.tile([P, D - HELP_LO], BF16, name="gamma_sb")
        beta_sb = const.tile([P, D - HELP_LO], BF16, name="beta_sb")
        nc.sync.dma_start(out=gamma_sb[:], in_=gamma[HELP_LO:D].partition_broadcast(P))
        nc.sync.dma_start(out=beta_sb[:], in_=beta[HELP_LO:D].partition_broadcast(P))

        def turn(dst, words, g, u):
            nc.tensor.transpose(dst, words[:, WORDS * g + u:WORDS * (g + 1):2], ident[:])

        def interleaved(bank):
            return bank.rearrange("p (a u) r -> p a r u", u=2)

        def cat_transposes(i):
            words = cat_raw[i][:].bitcast(F32)
            bank_a = work.tile([P, 4, P], F32, name="bank_a", tag="bank")
            for g in (0, 1):
                for u in (0, 1):
                    turn(bank_a[:, 2 * g + u, :], words, g, u)
            bank_b = work.tile([P, 4, P], F32, name="bank_b", tag="bank")
            for u in (0, 1):
                turn(bank_b[:, u, :], words, 2, u)
            return bank_a, bank_b

        def cat_copies(banks):
            bank_a, bank_b = banks
            grouped_a = grp.tile([P, 2, P, 4], BF16, name="grouped_a", tag="grouped_a", align_bytes=64)
            grouped_b = grp.tile([P, 1, P, 4], BF16, name="grouped_b", tag="grouped_b", align_bytes=64)
            nc.scalar.copy(out=grouped_a[:].bitcast(F32), in_=interleaved(bank_a[:]))
            nc.scalar.copy(out=grouped_b[:].bitcast(F32), in_=interleaved(bank_b[:, 0:2, :]))
            return grouped_a, grouped_b

        def cat_quantize(grouped):
            grouped_a, grouped_b = grouped
            codes_a = codes.tile([P, 2 * P], U32, name="codes_a", tag="codes_a", align_bytes=64)
            scales_a = codes.tile([P, 2 * P], U8, name="scales_a", tag="scales_a", align_bytes=64)
            codes_b = codes.tile([P, P], U32, name="codes_b", tag="codes_b", align_bytes=64)
            scales_b = codes.tile([P, P], U8, name="scales_b", tag="scales_b", align_bytes=64)
            nc.vector.quantize_mx(out=codes_a[:].bitcast(FP8X4), scales=scales_a[:], in_=grouped_a[:].rearrange("p g r t -> p (g r t)"))
            nc.vector.quantize_mx(out=codes_b[:].bitcast(FP8X4), scales=scales_b[:], in_=grouped_b[:].rearrange("p g r t -> p (g r t)"))
            return ((codes_a[:, 0:P], scales_a[:, 0:P]), (codes_a[:, P:2 * P], scales_a[:, P:2 * P]), (codes_b[:], scales_b[:]))

        w_codes = [wkeep.tile([P, D], U32, name="w_codes%d" % g, align_bytes=64) for g in range(PASSES)]
        w_scales = [wkeep.tile([P, D], U8, name="w_scales%d" % g, align_bytes=64) for g in range(PASSES)]

        def w_pair(pair, between=None, before_quantize=None):
            banks = [work.tile([P, 4, P], F32, name="bank_w%d" % g, tag="bank") for g in range(PASSES)]
            for half in (0, 1):
                words = wo_raw[2 * pair + half][:].bitcast(F32)
                for g in range(PASSES):
                    for u in (0, 1):
                        turn(banks[g][:, 2 * half + u, :], words, g, u)
                if half == 0 and between is not None:
                    between()
            grouped = [grp.tile([P, 2, P, 4], BF16, name="grouped_w%d" % g, tag="grouped_w", bufs=4, align_bytes=64) for g in range(PASSES)]
            for g in range(PASSES):
                nc.scalar.copy(out=grouped[g][:].bitcast(F32), in_=interleaved(banks[g][:]))
            cols = slice(pair * 2 * P, (pair + 1) * 2 * P)
            if before_quantize is not None:
                before_quantize()
            for g in range(PASSES):
                nc.vector.quantize_mx(out=w_codes[g][:, cols].bitcast(FP8X4), scales=w_scales[g][:, cols], in_=grouped[g][:].rearrange("p h r t -> p (h r t)"))

        cat_mx = {}
        sum_main = {}
        sum_rest = {}

        def mx_group(i, lo, hi, acc):
            for g in range(PASSES):
                nc.tensor.matmul_mx(
                    out=acc,
                    lhsT=cat_mx[i][g][0].bitcast(FP8X4),
                    lhsT_scale=cat_mx[i][g][1],
                    rhs=w_codes[g][:, lo:hi].bitcast(FP8X4),
                    rhs_scale=w_scales[g][:, lo:hi],
                    start=(g == 0),
                    stop=(g == PASSES - 1),
                )

        def mx_main(i):
            bank = work.tile([P, MAIN], F32, name="bank_main", tag="bank")
            sum_main[i] = bank[:]
            mx_group(i, 0, MAIN, sum_main[i])

        def mx_rest(i):
            bank = work.tile([P, REST], F32, name="bank_rest", tag="bank")
            sum_rest[i] = bank[:]
            mx_group(i, MAIN, D, sum_rest[i])

        gamma_ps = pconst.tile([P, D], BF16, name="gamma_ps")
        beta_ps = pconst.tile([P, D], BF16, name="beta_ps")
        bias_sb = const.tile([P, D], BF16, name="bias_sb")
        res_bias = [raw.tile([P, D], F32, name="res_bias%d" % i) for i in range(N_TILES)]

        def spread(dst, c):
            nc.tensor.matmul(out=dst[:, 0:MAIN], lhsT=ones[:], rhs=vec_rows[c][:, 0:MAIN], start=True, stop=True)
            nc.tensor.matmul(out=dst[:, MAIN:D], lhsT=ones[:], rhs=vec_rows[c][:, MAIN:D], start=True, stop=True)

        def warm_up():
            scratch = work.tile([P, MAIN], F32, name="scratch", tag="bank")
            for w in range(WARM_UPS):
                nc.tensor.matmul(out=scratch[:, 0:P], lhsT=ident[:], rhs=ident[:], start=True, stop=True)

        def bias_spread():
            bias_ps = work.tile([P, D], BF16, name="bias_ps", tag="bank")
            spread(bias_ps, 0)
            nc.scalar.copy(out=bias_sb[:], in_=bias_ps[:])
            nc.vector.tensor_tensor(out=res_bias[0][:], in0=bias_ps[:], in1=res_raw[0][:], op=ALU.add)

        def pool_res_bias(i):
            token = small.tile([P, 1], U32, name="token", tag="token")
            nc.gpsimd.tensor_copy(out=token[:], in_=cat_mx[i][PASSES - 1][0][:, 0:1])
            nc.gpsimd.tensor_tensor(out=res_bias[i][:], in0=res_raw[i][:], in1=bias_sb[:], op=ALU.add)

        y = {}
        row_sums = {}
        neg_mean = {}
        rstd = {}
        scaled = {}
        result = {}

        def add_residual(i):
            y[i] = epi.tile([P, D], F32, name="y", tag="y")
            row_sums[i] = small.tile([P, 2], F32, name="row_sums", tag="row_sums")
            nc.vector.scalar_tensor_tensor(out=y[i][:, 0:MAIN], in0=sum_main[i], scalar=1.0, in1=res_bias[i][:, 0:MAIN], op0=ALU.mult, op1=ALU.add, accum_out=row_sums[i][:, 0:1])
            nc.vector.scalar_tensor_tensor(out=y[i][:, MAIN:D], in0=sum_rest[i], scalar=1.0, in1=res_bias[i][:, MAIN:D], op0=ALU.mult, op1=ALU.add, accum_out=row_sums[i][:, 1:2])

        def mean(i):
            neg_mean[i] = small.tile([P, 1], F32, name="neg_mean", tag="neg_mean")
            unused = small.tile([P, 2], F32, name="unused2", tag="unused2")
            nc.scalar.activation(out=unused[:], in_=row_sums[i][:], func=ACT.Copy, scale=-1.0 / D, accum_out=neg_mean[i][:, 0:1])

        def variance(i):
            unused = epi.tile([P, D], BF16, name="unused", tag="unused")
            squares = small.tile([P, 1], F32, name="squares", tag="squares")
            nc.scalar.activation(out=unused[:], in_=y[i][:], func=ACT.Square, bias=neg_mean[i][:, 0:1], scale=1.0, accum_out=squares[:, 0:1])
            rstd[i] = small.tile([P, 1], F32, name="rstd", tag="rstd")
            nc.scalar.activation(out=rstd[i][:], in_=squares[:], func=ACT.Abs_reciprocal_sqrt, bias=eps_col[:, 0:1], scale=1.0 / D)

        def times_gamma(i):
            scaled[i] = epi.tile([P, D], F32, name="scaled", tag="scaled")
            hi = HELP_LO if i in HELPED else D
            nc.vector.scalar_tensor_tensor(out=scaled[i][:, 0:hi], in0=y[i][:, 0:hi], scalar=neg_mean[i][:, 0:1], in1=gamma_ps[:, 0:hi], op0=ALU.add, op1=ALU.mult)

        def plus_beta(i, lo, hi):
            if lo == 0:
                result[i] = epi.tile([P, D], F32, name="result", tag="result")
            nc.vector.scalar_tensor_tensor(out=result[i][:, lo:hi], in0=scaled[i][:, lo:hi], scalar=rstd[i][:, 0:1], in1=beta_ps[:, lo:hi], op0=ALU.mult, op1=ALU.add)
            nc.sync.dma_start(out=out0_hbm[i * P:(i + 1) * P, lo:hi], in_=result[i][:, lo:hi])

        def pool_help(i):
            normed = epi.tile([P, D - HELP_LO], F32, name="normed", tag="normed", bufs=2)
            gained = epi.tile([P, D - HELP_LO], F32, name="gained", tag="gained", bufs=2)
            nc.gpsimd.tensor_scalar(out=normed[:], in0=y[i][:, HELP_LO:D], scalar1=neg_mean[i][:, 0:1], scalar2=rstd[i][:, 0:1], op0=ALU.add, op1=ALU.mult)
            nc.gpsimd.tensor_tensor(out=gained[:], in0=normed[:], in1=gamma_sb[:], op=ALU.mult)
            nc.gpsimd.tensor_tensor(out=result[i][:, HELP_LO:D], in0=gained[:], in1=beta_sb[:], op=ALU.add)
            nc.sync.dma_start(out=out0_hbm[i * P:(i + 1) * P, HELP_LO:D], in_=result[i][:, HELP_LO:D])

        def cast(i, lo, hi, on_vector):
            fp8 = epi.tile([P, hi - lo], FP8, name="fp8", tag="fp8", bufs=8)
            if on_vector:
                nc.vector.tensor_scalar(out=fp8[:], in0=result[i][:, lo:hi], scalar1=Y_SCALE, scalar2=None, op0=ALU.mult, saturate=False)
            else:
                nc.scalar.activation(out=fp8[:], in_=result[i][:, lo:hi], func=ACT.Copy, scale=Y_SCALE, saturate=False)
            return fp8

        def store_bytes(i, lo, hi, fp8):
            nc.sync.dma_start(out=out1_hbm[i * P:(i + 1) * P, lo:hi], in_=fp8[:].bitcast(U8))

        warm_up()
        grouped_0 = cat_copies(cat_transposes(0))
        cat_mx[0] = cat_quantize(grouped_0)
        w_pair(0, bias_spread)
        spread(gamma_ps, 1)
        w_pair(1)
        w_pair(2, lambda: spread(beta_ps, 2), lambda: nc.vector.tensor_tensor(out=res_bias[1][:], in0=res_raw[1][:], in1=bias_sb[:], op=ALU.add))
        banks_1 = cat_transposes(1)
        mx_main(0)
        mx_rest(0)
        banks_2 = cat_transposes(2)
        grouped = {1: cat_copies(banks_1)}

        for i in range(N_TILES + 1):
            if i < N_TILES:
                add_residual(i)
            if i == 0:
                cat_mx[1] = cat_quantize(grouped[1])
            if i + 1 < N_TILES:
                mx_main(i + 1)
                mx_rest(i + 1)
            if i + 3 < N_TILES:
                banks_ahead = cat_transposes(i + 3)
            if i < N_TILES:
                mean(i)
            if i == 0:
                grouped[2] = cat_copies(banks_2)
            if 1 <= i < N_TILES:
                plus_beta(i - 1, 0, HELP_LO if i - 1 in HELPED else D)
            if i < N_TILES:
                variance(i)
            if 1 <= i < N_TILES:
                hi = HELP_LO if i - 1 in HELPED else D
                store_bytes(i - 1, 0, hi, cast(i - 1, 0, hi, False))
            if i - 1 in HELPED:
                pool_help(i - 1)
            if i - 2 in HELPED:
                store_bytes(i - 2, HELP_LO, D, cast(i - 2, HELP_LO, D, False))
            if i == N_TILES:
                plus_beta(i - 1, 0, LAST_SPLIT)
                fp8_first = cast(i - 1, 0, LAST_SPLIT, False)
                plus_beta(i - 1, LAST_SPLIT, D)
                store_bytes(i - 1, LAST_SPLIT, D, cast(i - 1, LAST_SPLIT, D, True))
                store_bytes(i - 1, 0, LAST_SPLIT, fp8_first)
            if i == 0:
                times_gamma(i)
            if i + 2 < N_TILES:
                cat_mx[i + 2] = cat_quantize(grouped[i + 2])
                pool_res_bias(i + 2)
            if 1 <= i < N_TILES:
                times_gamma(i)
            if i + 3 < N_TILES:
                grouped[i + 3] = cat_copies(banks_ahead)
